import numpy as np
import ml_dtypes


def mxq(x, axis, fmt="e4m3"):
    dtype, down = {"e4m3": (ml_dtypes.float8_e4m3fn, 7), "e5m2": (ml_dtypes.float8_e5m2, 14)}[fmt]
    v = np.moveaxis(np.asarray(x, np.float32).astype(ml_dtypes.bfloat16).astype(np.float64), axis, -1)
    blocks = v.reshape(v.shape[:-1] + (-1, 32))
    amax = np.abs(blocks).max(-1, keepdims=True)
    byte = np.maximum(np.where(amax > 0, np.frexp(amax)[1] - 1 + 127, 0) - down, 1)
    scale = np.exp2(byte - 127.0)
    codes = (blocks / scale).astype(np.float32).astype(dtype).astype(np.float64)
    return np.moveaxis((codes * scale).reshape(v.shape), -1, axis)


WIDE = False


def mx_kscale(k):
    if not WIDE:
        return np.ones(k)
    levels = np.array([10, -10, 5, -5, 0])
    a = np.random.permutation(np.resize(levels, k // 512 * 4)).reshape(k // 512, 4)
    idx = np.arange(k)
    return np.exp2(a[idx // 512, idx % 128 // 32])


BF16 = ml_dtypes.bfloat16


def bf(x):
    return np.asarray(x, np.float32).astype(BF16)


def f64(x):
    return np.asarray(x).astype(np.float64)


B, N, DIM, HEADS, WIN, FF, TIME_DIM = 1, 1536, 1024, 8, 512, 2048, 512
HD = DIM // HEADS
EPS = 1e-5


def layernorm(x, g, b):
    mu = x.mean(-1, keepdims=True)
    var = np.square(x - mu).mean(-1, keepdims=True)
    return (x - mu) / np.sqrt(var + EPS) * g + b


def setup_inputs():
    s = mx_kscale(DIM)
    return {
        "x": bf(np.random.standard_normal((B, N, DIM)) * (0.5 + 1.5 * np.random.random((B, N, 1))) + 0.5 * np.random.standard_normal((B, N, 1))),
        "t_scale": bf(np.random.standard_normal((B, DIM)) * 0.5),
        "t_shift": bf(np.random.standard_normal((B, DIM)) * 0.5 * s),
        "ln1_g": bf((1.0 + 0.1 * np.random.standard_normal(DIM)) * s),
        "ln1_b": bf(0.1 * np.random.standard_normal(DIM) * s),
        "qkv_w": bf(np.random.standard_normal((DIM, 3 * DIM)) * 1.2 / np.sqrt(DIM) / s[:, None]),
        "qkv_b": bf(np.random.standard_normal(3 * DIM) * 0.2),
    }


def reference(x, t_scale, t_shift, ln1_g, ln1_b, qkv_w, qkv_b):
    x_norm = layernorm(f64(x), f64(ln1_g), f64(ln1_b)) * (1.0 + f64(t_scale)[:, None, :]) + f64(t_shift)[:, None, :]
    qkv = (mxq(x_norm, 2, "e4m3") @ mxq(f64(qkv_w), 0, "e4m3")) + f64(qkv_b)
    return qkv.reshape(B, N, 3, HEADS, HD).transpose(2, 0, 3, 1, 4)

@@ -1,0 +1,221 @@
+from contextlib import ExitStack
+
+import concourse.mybir as mybir
+from concourse.masks import make_identity
+
+F32 = mybir.dt.float32
+BF16 = mybir.dt.bfloat16
+U32 = mybir.dt.uint32
+U8 = mybir.dt.uint8
+FP8X4 = mybir.dt.float8_e4m3fn_x4
+ALU = mybir.AluOpType
+ACT = mybir.ActivationFunctionType
+
+P = 128
+TOKENS = 1536
+DIM = 1024
+COLS = 3072
+HEAD_DIM = 128
+EPS = 1e-5
+
+PACK = 4
+K_PASS = P * PACK
+PASSES = DIM // K_PASS
+K_CHUNKS = DIM // P
+TILES = TOKENS // P
+GROUP_TILES = 4
+GROUPS = TILES // GROUP_TILES
+GROUP_TOKENS = GROUP_TILES * P
+N_COLS = 512
+COL_GROUPS = COLS // N_COLS
+GROUP_HEADS = N_COLS // HEAD_DIM
+LOAD_COLS = 1024
+LOADS = COLS // LOAD_COLS
+BN_WIDTH = 512
+BN_PARTS = DIM // BN_WIDTH
+BN_STATS = 6
+RUN = 4
+VECTOR_TILES = 3
+
+FLOPS = 2 * TOKENS * DIM * COLS
+
+
+def tile_localattentionblock_pa_kernel(
+    tc, x, t_scale, t_shift, ln1_g, ln1_b, qkv_w, qkv_b, out
+):
+    nc = tc.nc
+
+    x_view = x.rearrange("b (p t) k -> p (b t) k", t=TILES)
+    out_view = out.rearrange("j b h (p t) d -> p (j b h) t d", t=TILES)
+    w_view = qkv_w.rearrange("(g t p) n -> g p t n", t=PACK, p=P)
+
+    with ExitStack() as ctx:
+        keep = ctx.enter_context(tc.tile_pool(name="keep", bufs=1))
+        small = ctx.enter_context(tc.tile_pool(name="small", bufs=2 * GROUP_TILES))
+        xhat_pool = ctx.enter_context(tc.tile_pool(name="xhat_pool", bufs=2 * GROUP_TILES))
+        xn_pool = ctx.enter_context(tc.tile_pool(name="xn_pool", bufs=2))
+        grouped_pool = ctx.enter_context(tc.tile_pool(name="grouped_pool", bufs=4))
+        stage_pool = ctx.enter_context(tc.tile_pool(name="stage_pool", bufs=4))
+        xt_psum = ctx.enter_context(tc.psum_pool(name="xt_psum", bufs=4))
+        acc_psum = ctx.enter_context(tc.psum_pool(name="acc_psum", bufs=4))
+
+        neg_half = keep.tile([P, 1], F32, name="neg_half")
+        nc.vector.memset(neg_half[:], -0.5)
+        ident = keep.tile([P, P], F32, name="ident")
+        make_identity(nc, ident[:])
+
+        x_sb = [keep.tile([P, DIM], BF16, name="x_sb%d" % t) for t in range(TILES)]
+        w_raw = [
+            [keep.tile([P, PACK, LOAD_COLS], BF16, name="w_raw%d_%d" % (g, l)) for l in range(LOADS)]
+            for g in range(PASSES)
+        ]
+        bias = keep.tile([P, COLS], BF16, name="bias")
+
+        def load_x(group):
+            for t in range(group * GROUP_TILES, (group + 1) * GROUP_TILES):
+                nc.sync.dma_start(out=x_sb[t][:], in_=x_view[:, t, :])
+
+        def load_w(l):
+            for g in range(PASSES):
+                nc.sync.dma_start(
+                    out=w_raw[g][l][:], in_=w_view[g, :, :, l * LOAD_COLS : (l + 1) * LOAD_COLS]
+                )
+
+        vec_rows = keep.tile([P, P], BF16, name="vec_rows")
+        nc.vector.memset(vec_rows[:], 0.0)
+        vectors = [
+            ln1_g.rearrange("(r c) -> r c", c=P),
+            ln1_b.rearrange("(r c) -> r c", c=P),
+            t_scale.rearrange("b (r c) -> (b r) c", c=P),
+            t_shift.rearrange("b (r c) -> (b r) c", c=P),
+        ]
+        for v in range(len(vectors)):
+            nc.scalar.dma_start(out=vec_rows[v * K_CHUNKS : (v + 1) * K_CHUNKS, :], in_=vectors[v])
+        load_x(0)
+        load_w(0)
+        load_x(1)
+        load_x(2)
+        nc.sync.dma_start(out=bias[:], in_=qkv_b.partition_broadcast(P))
+        load_w(1)
+        load_w(2)
+
+        vec_f32 = keep.tile([P, P], F32, name="vec_f32")
+        nc.vector.tensor_copy(out=vec_f32[:], in_=vec_rows[:])
+        vec_t = xt_psum.tile([P, GROUP_TOKENS], F32, name="xt")
+        nc.tensor.transpose(vec_t[:, 0:P], vec_f32[:], ident[:])
+        one_plus = keep.tile([P, K_CHUNKS], F32, name="one_plus")
+        gain = keep.tile([P, K_CHUNKS], F32, name="gain")
+        shift = keep.tile([P, K_CHUNKS], F32, name="shift")
+        nc.vector.tensor_scalar_add(out=one_plus[:], in0=vec_t[:, 2 * K_CHUNKS : 3 * K_CHUNKS], scalar1=1.0)
+        nc.vector.tensor_tensor(out=gain[:], in0=vec_t[:, 0:K_CHUNKS], in1=one_plus[:], op=ALU.mult)
+        nc.vector.tensor_tensor(out=shift[:], in0=vec_t[:, K_CHUNKS : 2 * K_CHUNKS], in1=one_plus[:], op=ALU.mult)
+        nc.vector.tensor_tensor(out=shift[:], in0=vec_t[:, 3 * K_CHUNKS : 4 * K_CHUNKS], in1=shift[:], op=ALU.add)
+
+        x_codes = [keep.tile([P, PASSES, GROUP_TOKENS], U32, name="x_codes%d" % g, align_bytes=64) for g in range(GROUPS)]
+        x_scales = [keep.tile([P, PASSES, GROUP_TOKENS], U8, name="x_scales%d" % g, align_bytes=64) for g in range(GROUPS)]
+        w_codes = [keep.tile([P, PASSES, N_COLS], U32, name="w_codes%d" % c, align_bytes=64) for c in range(COL_GROUPS)]
+        w_scales = [keep.tile([P, PASSES, N_COLS], U8, name="w_scales%d" % c, align_bytes=64) for c in range(COL_GROUPS)]
+
+        def regroup(copy, rows):
+            grouped = grouped_pool.tile([P, N_COLS, PACK], BF16, name="grouped", align_bytes=64)
+            copy(
+                out=grouped[:].rearrange("p (c i) t -> p c t i", i=RUN),
+                in_=rows.rearrange("p t (c i) -> p c t i", i=RUN),
+            )
+            return grouped
+
+        def quantise(grouped, codes, scales):
+            nc.vector.quantize_mx(
+                out=codes.bitcast(FP8X4), scales=scales, in_=grouped[:].rearrange("p n t -> p (n t)")
+            )
+
+        def normalise(group):
+            xhat = []
+            for t in range(group * GROUP_TILES, (group + 1) * GROUP_TILES):
+                stats = small.tile([P, BN_PARTS, BN_STATS], F32, name="stats")
+                for h in range(BN_PARTS):
+                    nc.vector.bn_stats(out=stats[:, h, :], in_=x_sb[t][:, h * BN_WIDTH : (h + 1) * BN_WIDTH])
+                mean_var = small.tile([P, 2], F32, name="mean_var")
+                nc.vector.bn_aggr(out=mean_var[:], in_=stats[:].rearrange("p h s -> p (h s)"))
+                var_eps = small.tile([P, 1], F32, name="var_eps")
+                nc.vector.tensor_scalar_add(out=var_eps[:], in0=mean_var[:, 1:2], scalar1=EPS)
+                rstd = small.tile([P, 1], F32, name="rstd")
+                nc.gpsimd.tensor_tensor(out=rstd[:], in0=var_eps[:], in1=neg_half[:], op=ALU.pow)
+                neg_mean_rstd = small.tile([P, 1], F32, name="neg_mean_rstd")
+                nc.gpsimd.tensor_scalar(
+                    out=neg_mean_rstd[:], in0=mean_var[:, 0:1], scalar1=rstd[:], scalar2=-1.0,
+                    op0=ALU.mult, op1=ALU.mult,
+                )
+                xhat_t = xhat_pool.tile([P, DIM], F32, name="xhat")
+                nc.gpsimd.tensor_scalar(
+                    out=xhat_t[:], in0=x_sb[t][:], scalar1=rstd[:], scalar2=neg_mean_rstd[:],
+                    op0=ALU.mult, op1=ALU.add,
+                )
+                xhat.append(xhat_t)
+            return xhat
+
+        def quantise_tokens(group, xhat):
+            xn = xn_pool.tile([P, K_CHUNKS, GROUP_TOKENS], BF16, name="xn")
+            for c in range(K_CHUNKS):
+                xt = xt_psum.tile([P, GROUP_TOKENS], F32, name="xt")
+                for i in range(GROUP_TILES):
+                    nc.tensor.transpose(xt[:, i * P : (i + 1) * P], xhat[i][:, c * P : (c + 1) * P], ident[:])
+                nc.scalar.activation(
+                    out=xn[:, c, :], in_=xt[:], func=ACT.Identity, scale=gain[:, c : c + 1], bias=shift[:, c : c + 1]
+                )
+            grouped = [regroup(nc.vector.tensor_copy, xn[:, g * PACK : (g + 1) * PACK, :]) for g in range(PASSES)]
+            for g in range(PASSES):
+                quantise(grouped[g], x_codes[group][:, g, :], x_scales[group][:, g, :])
+
+        def quantise_columns(c):
+            l = c * N_COLS // LOAD_COLS
+            first = c * N_COLS - l * LOAD_COLS
+            grouped = [regroup(nc.scalar.copy, w_raw[g][l][:, :, first : first + N_COLS]) for g in range(PASSES)]
+            for g in range(PASSES):
+                quantise(grouped[g], w_codes[c][:, g, :], w_scales[c][:, g, :])
+
+        def project(group, c):
+            stage = stage_pool.tile([P, GROUP_HEADS, GROUP_TILES, HEAD_DIM], F32, name="stage")
+            bias_heads = bias[:, c * N_COLS : (c + 1) * N_COLS].rearrange("p (h d) -> p h d", h=GROUP_HEADS)
+            for i in range(GROUP_TILES):
+                tokens = slice(i * P, (i + 1) * P)
+                acc = acc_psum.tile([P, N_COLS], F32, name="acc")
+                for g in range(PASSES):
+                    nc.tensor.matmul_mx(
+                        out=acc[:],
+                        lhsT=x_codes[group][:, g, tokens].bitcast(FP8X4),
+                        lhsT_scale=x_scales[group][:, g, tokens],
+                        rhs=w_codes[c][:, g, :].bitcast(FP8X4),
+                        rhs_scale=w_scales[c][:, g, :],
+                        start=(g == 0),
+                        stop=(g == PASSES - 1),
+                    )
+                acc_heads = acc[:].rearrange("p (h d) -> p h d", h=GROUP_HEADS)
+                if i < VECTOR_TILES:
+                    nc.vector.tensor_tensor(out=stage[:, :, i, :], in0=acc_heads, in1=bias_heads, op=ALU.add)
+                else:
+                    nc.scalar.copy(out=stage[:, :, i, :], in_=acc_heads)
+                    nc.gpsimd.tensor_tensor(out=stage[:, :, i, :], in0=stage[:, :, i, :], in1=bias_heads, op=ALU.add)
+            nc.sync.dma_start(
+                out=out_view[
+                    :,
+                    c * GROUP_HEADS : (c + 1) * GROUP_HEADS,
+                    group * GROUP_TILES : (group + 1) * GROUP_TILES,
+                    :,
+                ],
+                in_=stage[:],
+            )
+
+        xhat = {0: normalise(0)}
+        quantise_columns(0)
+        for step in range(COL_GROUPS):
+            if step < GROUPS:
+                quantise_tokens(step, xhat[step])
+            if step + 1 < GROUPS:
+                xhat[step + 1] = normalise(step + 1)
+            if step + 1 < COL_GROUPS:
+                quantise_columns(step + 1)
+            for group in range(min(step + 1, GROUPS)):
+                for c in range(step + 1):
+                    if max(group, c) == step:
+                        project(group, c)

@@ -59,8 +59,10 @@ def tile_localattentionblock_pa_kernel(
         xt_psum = ctx.enter_context(tc.psum_pool(name="xt_psum", bufs=4))
         acc_psum = ctx.enter_context(tc.psum_pool(name="acc_psum", bufs=4))
 
-        neg_half = keep.tile([P, 1], F32, name="neg_half")
-        nc.vector.memset(neg_half[:], -0.5)
+        one = keep.tile([P, 1], F32, name="one")
+        nc.vector.memset(one[:], 1.0)
+        warm = keep.tile([P, 1], F32, name="warm")
+        nc.scalar.activation(out=warm[:], in_=one[:], func=ACT.Sqrt)
         ident = keep.tile([P, P], F32, name="ident")
         make_identity(nc, ident[:])
 
@@ -139,17 +141,16 @@ def tile_localattentionblock_pa_kernel(
                 nc.vector.bn_aggr(out=mean_var[:], in_=stats[:].rearrange("p h s -> p (h s)"))
                 var_eps = small.tile([P, 1], F32, name="var_eps")
                 nc.vector.tensor_scalar_add(out=var_eps[:], in0=mean_var[:, 1:2], scalar1=EPS)
+                inv_var = small.tile([P, 1], F32, name="inv_var")
+                nc.vector.reciprocal(out=inv_var[:], in_=var_eps[:])
+                neg_mean = small.tile([P, 1], F32, name="neg_mean")
+                nc.vector.tensor_scalar_mul(out=neg_mean[:], in0=mean_var[:, 0:1], scalar1=-1.0)
                 rstd = small.tile([P, 1], F32, name="rstd")
-                nc.gpsimd.tensor_tensor(out=rstd[:], in0=var_eps[:], in1=neg_half[:], op=ALU.pow)
-                neg_mean_rstd = small.tile([P, 1], F32, name="neg_mean_rstd")
-                nc.gpsimd.tensor_scalar(
-                    out=neg_mean_rstd[:], in0=mean_var[:, 0:1], scalar1=rstd[:], scalar2=-1.0,
-                    op0=ALU.mult, op1=ALU.mult,
-                )
+                nc.scalar.activation(out=rstd[:], in_=inv_var[:], func=ACT.Sqrt)
                 xhat_t = xhat_pool.tile([P, DIM], F32, name="xhat")
                 nc.gpsimd.tensor_scalar(
-                    out=xhat_t[:], in0=x_sb[t][:], scalar1=rstd[:], scalar2=neg_mean_rstd[:],
-                    op0=ALU.mult, op1=ALU.add,
+                    out=xhat_t[:], in0=x_sb[t][:], scalar1=neg_mean[:], scalar2=rstd[:],
+                    op0=ALU.add, op1=ALU.mult,
                 )
                 xhat.append(xhat_t)
             return xhat

@@ -35,7 +35,7 @@ BN_WIDTH = 512
 BN_PARTS = DIM // BN_WIDTH
 BN_STATS = 6
 RUN = 4
-VECTOR_TILES = 3
+VECTOR_TILES = 4
 
 FLOPS = 2 * TOKENS * DIM * COLS
 

@@ -35,7 +35,6 @@ BN_WIDTH = 512
 BN_PARTS = DIM // BN_WIDTH
 BN_STATS = 6
 RUN = 4
-VECTOR_TILES = 4
 
 FLOPS = 2 * TOKENS * DIM * COLS
 
@@ -59,10 +58,10 @@ def tile_localattentionblock_pa_kernel(
         xt_psum = ctx.enter_context(tc.psum_pool(name="xt_psum", bufs=4))
         acc_psum = ctx.enter_context(tc.psum_pool(name="acc_psum", bufs=4))
 
-        one = keep.tile([P, 1], F32, name="one")
-        nc.vector.memset(one[:], 1.0)
+        eps = keep.tile([P, 1], F32, name="eps")
+        nc.vector.memset(eps[:], EPS)
         warm = keep.tile([P, 1], F32, name="warm")
-        nc.scalar.activation(out=warm[:], in_=one[:], func=ACT.Sqrt)
+        nc.scalar.activation(out=warm[:], in_=eps[:], func=ACT.Sqrt)
         ident = keep.tile([P, P], F32, name="ident")
         make_identity(nc, ident[:])
 
@@ -97,8 +96,8 @@ def tile_localattentionblock_pa_kernel(
         load_w(0)
         load_x(1)
         load_x(2)
-        nc.sync.dma_start(out=bias[:], in_=qkv_b.partition_broadcast(P))
         load_w(1)
+        nc.sync.dma_start(out=bias[:], in_=qkv_b.partition_broadcast(P))
         load_w(2)
 
         vec_f32 = keep.tile([P, P], F32, name="vec_f32")
@@ -139,14 +138,12 @@ def tile_localattentionblock_pa_kernel(
                     nc.vector.bn_stats(out=stats[:, h, :], in_=x_sb[t][:, h * BN_WIDTH : (h + 1) * BN_WIDTH])
                 mean_var = small.tile([P, 2], F32, name="mean_var")
                 nc.vector.bn_aggr(out=mean_var[:], in_=stats[:].rearrange("p h s -> p (h s)"))
-                var_eps = small.tile([P, 1], F32, name="var_eps")
-                nc.vector.tensor_scalar_add(out=var_eps[:], in0=mean_var[:, 1:2], scalar1=EPS)
-                inv_var = small.tile([P, 1], F32, name="inv_var")
-                nc.vector.reciprocal(out=inv_var[:], in_=var_eps[:])
                 neg_mean = small.tile([P, 1], F32, name="neg_mean")
-                nc.vector.tensor_scalar_mul(out=neg_mean[:], in0=mean_var[:, 0:1], scalar1=-1.0)
+                nc.scalar.mul(out=neg_mean[:], in_=mean_var[:, 0:1], mul=-1.0)
+                std = small.tile([P, 1], F32, name="std")
+                nc.scalar.activation(out=std[:], in_=mean_var[:, 1:2], func=ACT.Sqrt, bias=eps[:], scale=1.0)
                 rstd = small.tile([P, 1], F32, name="rstd")
-                nc.scalar.activation(out=rstd[:], in_=inv_var[:], func=ACT.Sqrt)
+                nc.vector.reciprocal(out=rstd[:], in_=std[:])
                 xhat_t = xhat_pool.tile([P, DIM], F32, name="xhat")
                 nc.gpsimd.tensor_scalar(
                     out=xhat_t[:], in0=x_sb[t][:], scalar1=neg_mean[:], scalar2=rstd[:],
@@ -192,11 +189,7 @@ def tile_localattentionblock_pa_kernel(
                         stop=(g == PASSES - 1),
                     )
                 acc_heads = acc[:].rearrange("p (h d) -> p h d", h=GROUP_HEADS)
-                if i < VECTOR_TILES:
-                    nc.vector.tensor_tensor(out=stage[:, :, i, :], in0=acc_heads, in1=bias_heads, op=ALU.add)
-                else:
-                    nc.scalar.copy(out=stage[:, :, i, :], in_=acc_heads)
-                    nc.gpsimd.tensor_tensor(out=stage[:, :, i, :], in0=stage[:, :, i, :], in1=bias_heads, op=ALU.add)
+                nc.vector.tensor_tensor(out=stage[:, :, i, :], in0=acc_heads, in1=bias_heads, op=ALU.add)
             nc.sync.dma_start(
                 out=out_view[
                     :,

@@ -34,6 +34,7 @@ LOADS = COLS // LOAD_COLS
 BN_WIDTH = 512
 BN_PARTS = DIM // BN_WIDTH
 BN_STATS = 6
+STAT_TILES = 2
 RUN = 4
 
 FLOPS = 2 * TOKENS * DIM * COLS
@@ -132,24 +133,28 @@ def tile_localattentionblock_pa_kernel(
 
         def normalise(group):
             xhat = []
-            for t in range(group * GROUP_TILES, (group + 1) * GROUP_TILES):
-                stats = small.tile([P, BN_PARTS, BN_STATS], F32, name="stats")
-                for h in range(BN_PARTS):
-                    nc.vector.bn_stats(out=stats[:, h, :], in_=x_sb[t][:, h * BN_WIDTH : (h + 1) * BN_WIDTH])
-                mean_var = small.tile([P, 2], F32, name="mean_var")
-                nc.vector.bn_aggr(out=mean_var[:], in_=stats[:].rearrange("p h s -> p (h s)"))
-                neg_mean = small.tile([P, 1], F32, name="neg_mean")
-                nc.scalar.mul(out=neg_mean[:], in_=mean_var[:, 0:1], mul=-1.0)
-                std = small.tile([P, 1], F32, name="std")
-                nc.scalar.activation(out=std[:], in_=mean_var[:, 1:2], func=ACT.Sqrt, bias=eps[:], scale=1.0)
-                rstd = small.tile([P, 1], F32, name="rstd")
+            for first in range(group * GROUP_TILES, (group + 1) * GROUP_TILES, STAT_TILES):
+                mean_var = small.tile([P, STAT_TILES, 2], F32, name="mean_var")
+                for i in range(STAT_TILES):
+                    stats = small.tile([P, BN_PARTS, BN_STATS], F32, name="stats")
+                    for h in range(BN_PARTS):
+                        nc.vector.bn_stats(
+                            out=stats[:, h, :], in_=x_sb[first + i][:, h * BN_WIDTH : (h + 1) * BN_WIDTH]
+                        )
+                    nc.vector.bn_aggr(out=mean_var[:, i, :], in_=stats[:].rearrange("p h s -> p (h s)"))
+                neg_mean = small.tile([P, STAT_TILES], F32, name="neg_mean")
+                nc.scalar.mul(out=neg_mean[:], in_=mean_var[:, :, 0], mul=-1.0)
+                std = small.tile([P, STAT_TILES], F32, name="std")
+                nc.scalar.activation(out=std[:], in_=mean_var[:, :, 1], func=ACT.Sqrt, bias=eps[:], scale=1.0)
+                rstd = small.tile([P, STAT_TILES], F32, name="rstd")
                 nc.vector.reciprocal(out=rstd[:], in_=std[:])
-                xhat_t = xhat_pool.tile([P, DIM], F32, name="xhat")
-                nc.gpsimd.tensor_scalar(
-                    out=xhat_t[:], in0=x_sb[t][:], scalar1=neg_mean[:], scalar2=rstd[:],
-                    op0=ALU.add, op1=ALU.mult,
-                )
-                xhat.append(xhat_t)
+                for i in range(STAT_TILES):
+                    xhat_t = xhat_pool.tile([P, DIM], F32, name="xhat")
+                    nc.gpsimd.tensor_scalar(
+                        out=xhat_t[:], in0=x_sb[first + i][:], scalar1=neg_mean[:, i : i + 1], scalar2=rstd[:, i : i + 1],
+                        op0=ALU.add, op1=ALU.mult,
+                    )
+                    xhat.append(xhat_t)
             return xhat
 
         def quantise_tokens(group, xhat):

from contextlib import ExitStack

import concourse.mybir as mybir
from concourse.masks import make_identity

F32 = mybir.dt.float32
BF16 = mybir.dt.bfloat16
U32 = mybir.dt.uint32
U8 = mybir.dt.uint8
FP8X4 = mybir.dt.float8_e4m3fn_x4
ALU = mybir.AluOpType
ACT = mybir.ActivationFunctionType

P = 128
TOKENS = 1536
DIM = 1024
COLS = 3072
HEAD_DIM = 128
EPS = 1e-5

PACK = 4
K_PASS = P * PACK
PASSES = DIM // K_PASS
K_CHUNKS = DIM // P
TILES = TOKENS // P
GROUP_TILES = 4
GROUPS = TILES // GROUP_TILES
GROUP_TOKENS = GROUP_TILES * P
N_COLS = 512
COL_GROUPS = COLS // N_COLS
GROUP_HEADS = N_COLS // HEAD_DIM
LOAD_COLS = 1024
LOADS = COLS // LOAD_COLS
BN_WIDTH = 512
BN_PARTS = DIM // BN_WIDTH
BN_STATS = 6
STAT_TILES = 2
RUN = 4

FLOPS = 2 * TOKENS * DIM * COLS


def tile_localattentionblock_pa_kernel(
    tc, x, t_scale, t_shift, ln1_g, ln1_b, qkv_w, qkv_b, out
):
    nc = tc.nc

    x_view = x.rearrange("b (p t) k -> p (b t) k", t=TILES)
    out_view = out.rearrange("j b h (p t) d -> p (j b h) t d", t=TILES)
    w_view = qkv_w.rearrange("(g t p) n -> g p t n", t=PACK, p=P)

    with ExitStack() as ctx:
        keep = ctx.enter_context(tc.tile_pool(name="keep", bufs=1))
        small = ctx.enter_context(tc.tile_pool(name="small", bufs=2 * GROUP_TILES))
        xhat_pool = ctx.enter_context(tc.tile_pool(name="xhat_pool", bufs=2 * GROUP_TILES))
        xn_pool = ctx.enter_context(tc.tile_pool(name="xn_pool", bufs=2))
        grouped_pool = ctx.enter_context(tc.tile_pool(name="grouped_pool", bufs=4))
        stage_pool = ctx.enter_context(tc.tile_pool(name="stage_pool", bufs=4))
        xt_psum = ctx.enter_context(tc.psum_pool(name="xt_psum", bufs=4))
        acc_psum = ctx.enter_context(tc.psum_pool(name="acc_psum", bufs=4))

        eps = keep.tile([P, 1], F32, name="eps")
        nc.vector.memset(eps[:], EPS)
        warm = keep.tile([P, 1], F32, name="warm")
        nc.scalar.activation(out=warm[:], in_=eps[:], func=ACT.Sqrt)
        ident = keep.tile([P, P], F32, name="ident")
        make_identity(nc, ident[:])

        x_sb = [keep.tile([P, DIM], BF16, name="x_sb%d" % t) for t in range(TILES)]
        w_raw = [
            [keep.tile([P, PACK, LOAD_COLS], BF16, name="w_raw%d_%d" % (g, l)) for l in range(LOADS)]
            for g in range(PASSES)
        ]
        bias = keep.tile([P, COLS], BF16, name="bias")

        def load_x(group):
            for t in range(group * GROUP_TILES, (group + 1) * GROUP_TILES):
                nc.sync.dma_start(out=x_sb[t][:], in_=x_view[:, t, :])

        def load_w(l):
            for g in range(PASSES):
                nc.sync.dma_start(
                    out=w_raw[g][l][:], in_=w_view[g, :, :, l * LOAD_COLS : (l + 1) * LOAD_COLS]
                )

        vec_rows = keep.tile([P, P], BF16, name="vec_rows")
        nc.vector.memset(vec_rows[:], 0.0)
        vectors = [
            ln1_g.rearrange("(r c) -> r c", c=P),
            ln1_b.rearrange("(r c) -> r c", c=P),
            t_scale.rearrange("b (r c) -> (b r) c", c=P),
            t_shift.rearrange("b (r c) -> (b r) c", c=P),
        ]
        for v in range(len(vectors)):
            nc.scalar.dma_start(out=vec_rows[v * K_CHUNKS : (v + 1) * K_CHUNKS, :], in_=vectors[v])
        load_x(0)
        load_w(0)
        load_x(1)
        load_x(2)
        load_w(1)
        nc.sync.dma_start(out=bias[:], in_=qkv_b.partition_broadcast(P))
        load_w(2)

        vec_f32 = keep.tile([P, P], F32, name="vec_f32")
        nc.vector.tensor_copy(out=vec_f32[:], in_=vec_rows[:])
        vec_t = xt_psum.tile([P, GROUP_TOKENS], F32, name="xt")
        nc.tensor.transpose(vec_t[:, 0:P], vec_f32[:], ident[:])
        one_plus = keep.tile([P, K_CHUNKS], F32, name="one_plus")
        gain = keep.tile([P, K_CHUNKS], F32, name="gain")
        shift = keep.tile([P, K_CHUNKS], F32, name="shift")
        nc.vector.tensor_scalar_add(out=one_plus[:], in0=vec_t[:, 2 * K_CHUNKS : 3 * K_CHUNKS], scalar1=1.0)
        nc.vector.tensor_tensor(out=gain[:], in0=vec_t[:, 0:K_CHUNKS], in1=one_plus[:], op=ALU.mult)
        nc.vector.tensor_tensor(out=shift[:], in0=vec_t[:, K_CHUNKS : 2 * K_CHUNKS], in1=one_plus[:], op=ALU.mult)
        nc.vector.tensor_tensor(out=shift[:], in0=vec_t[:, 3 * K_CHUNKS : 4 * K_CHUNKS], in1=shift[:], op=ALU.add)

        x_codes = [keep.tile([P, PASSES, GROUP_TOKENS], U32, name="x_codes%d" % g, align_bytes=64) for g in range(GROUPS)]
        x_scales = [keep.tile([P, PASSES, GROUP_TOKENS], U8, name="x_scales%d" % g, align_bytes=64) for g in range(GROUPS)]
        w_codes = [keep.tile([P, PASSES, N_COLS], U32, name="w_codes%d" % c, align_bytes=64) for c in range(COL_GROUPS)]
        w_scales = [keep.tile([P, PASSES, N_COLS], U8, name="w_scales%d" % c, align_bytes=64) for c in range(COL_GROUPS)]

        def regroup(copy, rows):
            grouped = grouped_pool.tile([P, N_COLS, PACK], BF16, name="grouped", align_bytes=64)
            copy(
                out=grouped[:].rearrange("p (c i) t -> p c t i", i=RUN),
                in_=rows.rearrange("p t (c i) -> p c t i", i=RUN),
            )
            return grouped

        def quantise(grouped, codes, scales):
            nc.vector.quantize_mx(
                out=codes.bitcast(FP8X4), scales=scales, in_=grouped[:].rearrange("p n t -> p (n t)")
            )

        def normalise(group):
            xhat = []
            for first in range(group * GROUP_TILES, (group + 1) * GROUP_TILES, STAT_TILES):
                mean_var = small.tile([P, STAT_TILES, 2], F32, name="mean_var")
                for i in range(STAT_TILES):
                    stats = small.tile([P, BN_PARTS, BN_STATS], F32, name="stats")
                    for h in range(BN_PARTS):
                        nc.vector.bn_stats(
                            out=stats[:, h, :], in_=x_sb[first + i][:, h * BN_WIDTH : (h + 1) * BN_WIDTH]
                        )
                    nc.vector.bn_aggr(out=mean_var[:, i, :], in_=stats[:].rearrange("p h s -> p (h s)"))
                neg_mean = small.tile([P, STAT_TILES], F32, name="neg_mean")
                nc.scalar.mul(out=neg_mean[:], in_=mean_var[:, :, 0], mul=-1.0)
                std = small.tile([P, STAT_TILES], F32, name="std")
                nc.scalar.activation(out=std[:], in_=mean_var[:, :, 1], func=ACT.Sqrt, bias=eps[:], scale=1.0)
                rstd = small.tile([P, STAT_TILES], F32, name="rstd")
                nc.vector.reciprocal(out=rstd[:], in_=std[:])
                for i in range(STAT_TILES):
                    xhat_t = xhat_pool.tile([P, DIM], F32, name="xhat")
                    nc.gpsimd.tensor_scalar(
                        out=xhat_t[:], in0=x_sb[first + i][:], scalar1=neg_mean[:, i : i + 1], scalar2=rstd[:, i : i + 1],
                        op0=ALU.add, op1=ALU.mult,
                    )
                    xhat.append(xhat_t)
            return xhat

        def quantise_tokens(group, xhat):
            xn = xn_pool.tile([P, K_CHUNKS, GROUP_TOKENS], BF16, name="xn")
            for c in range(K_CHUNKS):
                xt = xt_psum.tile([P, GROUP_TOKENS], F32, name="xt")
                for i in range(GROUP_TILES):
                    nc.tensor.transpose(xt[:, i * P : (i + 1) * P], xhat[i][:, c * P : (c + 1) * P], ident[:])
                nc.scalar.activation(
                    out=xn[:, c, :], in_=xt[:], func=ACT.Identity, scale=gain[:, c : c + 1], bias=shift[:, c : c + 1]
                )
            grouped = [regroup(nc.vector.tensor_copy, xn[:, g * PACK : (g + 1) * PACK, :]) for g in range(PASSES)]
            for g in range(PASSES):
                quantise(grouped[g], x_codes[group][:, g, :], x_scales[group][:, g, :])

        def quantise_columns(c):
            l = c * N_COLS // LOAD_COLS
            first = c * N_COLS - l * LOAD_COLS
            grouped = [regroup(nc.scalar.copy, w_raw[g][l][:, :, first : first + N_COLS]) for g in range(PASSES)]
            for g in range(PASSES):
                quantise(grouped[g], w_codes[c][:, g, :], w_scales[c][:, g, :])

        def project(group, c):
            stage = stage_pool.tile([P, GROUP_HEADS, GROUP_TILES, HEAD_DIM], F32, name="stage")
            bias_heads = bias[:, c * N_COLS : (c + 1) * N_COLS].rearrange("p (h d) -> p h d", h=GROUP_HEADS)
            for i in range(GROUP_TILES):
                tokens = slice(i * P, (i + 1) * P)
                acc = acc_psum.tile([P, N_COLS], F32, name="acc")
                for g in range(PASSES):
                    nc.tensor.matmul_mx(
                        out=acc[:],
                        lhsT=x_codes[group][:, g, tokens].bitcast(FP8X4),
                        lhsT_scale=x_scales[group][:, g, tokens],
                        rhs=w_codes[c][:, g, :].bitcast(FP8X4),
                        rhs_scale=w_scales[c][:, g, :],
                        start=(g == 0),
                        stop=(g == PASSES - 1),
                    )
                acc_heads = acc[:].rearrange("p (h d) -> p h d", h=GROUP_HEADS)
                nc.vector.tensor_tensor(out=stage[:, :, i, :], in0=acc_heads, in1=bias_heads, op=ALU.add)
            nc.sync.dma_start(
                out=out_view[
                    :,
                    c * GROUP_HEADS : (c + 1) * GROUP_HEADS,
                    group * GROUP_TILES : (group + 1) * GROUP_TILES,
                    :,
                ],
                in_=stage[:],
            )

        xhat = {0: normalise(0)}
        quantise_columns(0)
        for step in range(COL_GROUPS):
            if step < GROUPS:
                quantise_tokens(step, xhat[step])
            if step + 1 < GROUPS:
                xhat[step + 1] = normalise(step + 1)
            if step + 1 < COL_GROUPS:
                quantise_columns(step + 1)
            for group in range(min(step + 1, GROUPS)):
                for c in range(step + 1):
                    if max(group, c) == step:
                        project(group, c)
